import numpy as np
import ml_dtypes


def mxq(x, axis, fmt="e4m3"):
    dtype, down = {"e4m3": (ml_dtypes.float8_e4m3fn, 7), "e5m2": (ml_dtypes.float8_e5m2, 14)}[fmt]
    v = np.moveaxis(np.asarray(x, np.float32).astype(ml_dtypes.bfloat16).astype(np.float64), axis, -1)
    blocks = v.reshape(v.shape[:-1] + (-1, 32))
    amax = np.abs(blocks).max(-1, keepdims=True)
    byte = np.maximum(np.where(amax > 0, np.frexp(amax)[1] - 1 + 127, 0) - down, 1)
    scale = np.exp2(byte - 127.0)
    codes = (blocks / scale).astype(np.float32).astype(dtype).astype(np.float64)
    return np.moveaxis((codes * scale).reshape(v.shape), -1, axis)


WIDE = False


def mx_kscale(k):
    if not WIDE:
        return np.ones(k)
    levels = np.array([10, -10, 5, -5, 0])
    a = np.random.permutation(np.resize(levels, k // 512 * 4)).reshape(k // 512, 4)
    idx = np.arange(k)
    return np.exp2(a[idx // 512, idx % 128 // 32])


BF16 = ml_dtypes.bfloat16


def bf(x):
    return np.asarray(x, np.float32).astype(BF16)


def f64(x):
    return np.asarray(x).astype(np.float64)


B, N, DI, D, H, DO = 2, 512, 1024, 1024, 16, 1024
DH = D // H
SIG = 0.5


def time_concat(space):
    t = np.sqrt(1.0 + np.sum(space * space, axis=-1, keepdims=True))
    return np.concatenate([t, space], axis=-1)


def split_lift(space):
    return time_concat(space.reshape(B, N, H, DH).transpose(0, 2, 1, 3))


def setup_inputs():
    s = mx_kscale(DI)
    return {"x_space": bf(np.random.standard_normal((B, N, DI)) * s),
            "Wq": bf(np.random.standard_normal((D, DI)) * SIG / np.sqrt(DI) / s),
            "bq": bf(np.random.standard_normal(D) * 0.1),
            "Wk": bf(np.random.standard_normal((D, DI)) * SIG / np.sqrt(DI) / s),
            "bk": bf(np.random.standard_normal(D) * 0.1)}


def reference(x_space, Wq, bq, Wk, bk):
    xq = mxq(f64(x_space), 2, "e4m3")
    q = (xq @ mxq(f64(Wq), 1, "e4m3").T) + f64(bq)
    k = (xq @ mxq(f64(Wk), 1, "e4m3").T) + f64(bk)
    return split_lift(q), split_lift(k)

@@ -1,0 +1,192 @@
+from contextlib import ExitStack
+
+import concourse.mybir as mybir
+from concourse.masks import make_identity
+
+F32 = mybir.dt.float32
+BF16 = mybir.dt.bfloat16
+U32 = mybir.dt.uint32
+U8 = mybir.dt.uint8
+FP8X4 = mybir.dt.float8_e4m3fn_x4
+ACT = mybir.ActivationFunctionType
+ALU = mybir.AluOpType
+
+P = 128
+BATCH, TOKENS, K = 2, 512, 1024
+FEATURES, HEAD_DIM = 1024, 64
+LIFTED = HEAD_DIM + 1
+PACK = 4
+K_PASS = P * PACK
+PASSES = K // K_PASS
+HALVES = 2
+ROW_WORDS = K // 2
+BLOCKS = 2
+UNIT_ROWS = BLOCKS * P
+J = BATCH * TOKENS // P
+X_UNITS = J // BLOCKS
+CHUNK_HEADS = UNIT_ROWS // HEAD_DIM
+W_UNITS = FEATURES // UNIT_ROWS
+CHUNKS = 2 * W_UNITS
+BANK = 512
+
+FLOPS = 2 * BATCH * TOKENS * K * 2 * FEATURES
+
+
+def tile_lorentzmultiheadattention_pa_kernel(tc, x_space, Wq, bq, Wk, bk, out_0, out_1):
+    nc = tc.nc
+    weights = (Wq, Wk)
+    outputs = (out_0, out_1)
+
+    with ExitStack() as ctx:
+        consts = ctx.enter_context(tc.tile_pool(name="consts", bufs=1))
+        raw_pool = ctx.enter_context(tc.tile_pool(name="raw", bufs=1))
+        mx_pool = ctx.enter_context(tc.tile_pool(name="mx", bufs=1))
+        stage = ctx.enter_context(tc.tile_pool(name="stage", bufs=3))
+        out_pool = ctx.enter_context(tc.tile_pool(name="outp", bufs=CHUNKS))
+        scratch = ctx.enter_context(tc.tile_pool(name="scratch", bufs=4))
+        flip_psum = ctx.enter_context(tc.psum_pool(name="flip", bufs=4))
+        acc_psum = ctx.enter_context(tc.psum_pool(name="acc", bufs=4))
+        ctx.enter_context(tc.manual_schedule())
+
+        one = consts.tile([P, 1], F32)
+        nc.vector.memset(one[:], 1.0)
+        root = consts.tile([P, 1], F32)
+        nc.scalar.activation(out=root[:], in_=one[:], func=ACT.Sqrt)
+        ident = consts.tile([P, P], F32)
+        make_identity(nc, ident[:])
+        ones = consts.tile([P, P], BF16)
+        nc.vector.memset(ones[:], 1.0)
+        bias_rows = consts.tile([P, 2 * FEATURES], BF16)
+        nc.vector.memset(bias_rows[:], 0.0)
+
+        def load_x(unit):
+            raw = raw_pool.tile([P, BLOCKS * K], BF16, name="raw_x%d" % unit)
+            for b in range(BATCH):
+                rows = x_space[b].rearrange("(p j) k -> p (j k)", j=J)
+                nc.sync.dma_start(
+                    out=raw[b:P:BATCH, :],
+                    in_=rows[:, unit * BLOCKS * K : (unit + 1) * BLOCKS * K],
+                )
+            return raw
+
+        def load_w(chunk):
+            raw = raw_pool.tile([P, BLOCKS * K], BF16, name="raw_w%d" % chunk)
+            rows = weights[chunk // W_UNITS].rearrange("(c b r) k -> c r b k", b=BLOCKS, r=P)
+            nc.sync.dma_start(
+                out=raw[:].rearrange("p (b k) -> p b k", b=BLOCKS),
+                in_=rows[chunk % W_UNITS],
+            )
+            return raw
+
+        raw_x = [None] * X_UNITS
+        raw_w = [None] * CHUNKS
+        raw_x[0] = load_x(0)
+        raw_w[0] = load_w(0)
+        nc.sync.dma_start(out=bias_rows[0:1, 0:FEATURES], in_=bq.unsqueeze(0))
+        nc.sync.dma_start(out=bias_rows[0:1, FEATURES : 2 * FEATURES], in_=bk.unsqueeze(0))
+        raw_x[1] = load_x(1)
+        raw_x[2] = load_x(2)
+        raw_w[1] = load_w(1)
+        raw_x[3] = load_x(3)
+        for chunk in range(2, CHUNKS):
+            raw_w[chunk] = load_w(chunk)
+
+        def flip(raw, share_with_scalar):
+            words = raw[:].bitcast(F32)
+            grouped = stage.tile([P, PASSES * UNIT_ROWS * PACK], BF16, align_bytes=64, tag="grouped")
+            grouped_words = grouped[:].bitcast(F32).rearrange(
+                "p (g b r u) -> p g b r u", g=PASSES, b=BLOCKS, u=HALVES
+            )
+            for b in range(BLOCKS):
+                flipped = flip_psum.tile([P, PASSES, HALVES, P], F32, tag="flip")
+                for g in range(PASSES):
+                    for u in range(HALVES):
+                        first = b * ROW_WORDS + (g * HALVES + u) * P
+                        nc.tensor.transpose(flipped[:, g, u, :], words[:, first : first + P], ident[:])
+                source = flipped[:].rearrange("p g u r -> p g r u")
+                if share_with_scalar and b == 0:
+                    nc.scalar.copy(out=grouped_words[:, :, b, :, :], in_=source)
+                else:
+                    nc.vector.tensor_copy(out=grouped_words[:, :, b, :, :], in_=source)
+            return grouped
+
+        def quantise(grouped, name):
+            codes = mx_pool.tile([P, PASSES, UNIT_ROWS], U32, align_bytes=64, name="codes_" + name)
+            scales = mx_pool.tile([P, PASSES, UNIT_ROWS], U8, align_bytes=64, name="scales_" + name)
+            nc.vector.quantize_mx(
+                out=codes[:].rearrange("p g r -> p (g r)").bitcast(FP8X4),
+                scales=scales[:].rearrange("p g r -> p (g r)"),
+                in_=grouped[:],
+            )
+            return codes, scales
+
+        x_mx = [None] * X_UNITS
+        w_mx = [None] * CHUNKS
+        x_mx[0] = quantise(flip(raw_x[0], True), "x0")
+        w_mx[0] = quantise(flip(raw_w[0], True), "w0")
+
+        bias = consts.tile([P, 2 * FEATURES], F32)
+        for q in range(2 * FEATURES // BANK):
+            spread = acc_psum.tile([P, BANK], F32, tag="acc")
+            cols = slice(q * BANK, (q + 1) * BANK)
+            nc.tensor.matmul(out=spread[:], lhsT=ones[:], rhs=bias_rows[:, cols], start=True, stop=True)
+            nc.scalar.copy(out=bias[:, cols], in_=spread[:])
+
+        for chunk in range(CHUNKS):
+            lifted = out_pool.tile([P, CHUNK_HEADS, J, LIFTED], F32, tag="lifted")
+            norms = out_pool.tile([P, CHUNK_HEADS, J], F32, tag="norms")
+            bias_chunk = bias[:, chunk * UNIT_ROWS : (chunk + 1) * UNIT_ROWS].rearrange(
+                "p (h d) -> p h d", d=HEAD_DIM
+            )
+            w_codes, w_scales = w_mx[chunk]
+            for unit in range(X_UNITS):
+                next_x = chunk == 0 and unit + 1 < X_UNITS
+                next_w = unit == 1 and chunk + 1 < CHUNKS
+                if next_x:
+                    grouped_x = flip(raw_x[unit + 1], True)
+                if next_w:
+                    grouped_w = flip(raw_w[chunk + 1], chunk == 0)
+
+                x_codes, x_scales = x_mx[unit]
+                acc = acc_psum.tile([P, BLOCKS, UNIT_ROWS], F32, tag="acc")
+                for b in range(BLOCKS):
+                    tokens = slice(b * P, (b + 1) * P)
+                    for g in range(PASSES):
+                        nc.tensor.matmul_mx(
+                            out=acc[:, b, :],
+                            lhsT=x_codes[:, g, tokens].bitcast(FP8X4),
+                            lhsT_scale=x_scales[:, g, tokens],
+                            rhs=w_codes[:, g, :].bitcast(FP8X4),
+                            rhs_scale=w_scales[:, g, :],
+                            start=(g == 0),
+                            stop=(g == PASSES - 1),
+                        )
+                j0 = unit * BLOCKS
+                nc.vector.tensor_tensor(
+                    out=lifted[:, :, j0 : j0 + BLOCKS, 1:LIFTED],
+                    in0=acc[:].rearrange("p b (h d) -> p h b d", d=HEAD_DIM),
+                    in1=bias_chunk.unsqueeze(2).to_broadcast([P, CHUNK_HEADS, BLOCKS, HEAD_DIM]),
+                    op=ALU.add,
+                )
+                squares = scratch.tile([P, CHUNK_HEADS, BLOCKS, HEAD_DIM], F32, tag="squares")
+                for h in range(CHUNK_HEADS):
+                    for b in range(BLOCKS):
+                        nc.scalar.activation(
+                            out=squares[:, h, b, :],
+                            in_=lifted[:, h, j0 + b, 1:LIFTED],
+                            func=ACT.Square,
+                            accum_out=norms[:, h, j0 + b : j0 + b + 1],
+                        )
+                if next_x:
+                    x_mx[unit + 1] = quantise(grouped_x, "x%d" % (unit + 1))
+                if next_w:
+                    w_mx[chunk + 1] = quantise(grouped_w, "w%d" % (chunk + 1))
+            nc.scalar.activation(out=lifted[:, :, :, 0], in_=norms[:], func=ACT.Sqrt, bias=1.0)
+            h0 = (chunk % W_UNITS) * CHUNK_HEADS
+            for b in range(BATCH):
+                nc.sync.dma_start(
+                    out=outputs[chunk // W_UNITS][b, h0 : h0 + CHUNK_HEADS].rearrange(
+                        "h (p j) c -> p h (j c)", j=J
+                    ),
+                    in_=lifted[b:P:BATCH].rearrange("p h j c -> p h (j c)"),
+                )

@@ -27,6 +27,8 @@ X_UNITS = J // BLOCKS
 CHUNK_HEADS = UNIT_ROWS // HEAD_DIM
 W_UNITS = FEATURES // UNIT_ROWS
 CHUNKS = 2 * W_UNITS
+SCALAR_HEADS = 2
+STEPS = CHUNKS * X_UNITS
 BANK = 512
 
 FLOPS = 2 * BATCH * TOKENS * K * 2 * FEATURES
@@ -35,13 +37,14 @@ FLOPS = 2 * BATCH * TOKENS * K * 2 * FEATURES
 def tile_lorentzmultiheadattention_pa_kernel(tc, x_space, Wq, bq, Wk, bk, out_0, out_1):
     nc = tc.nc
     weights = (Wq, Wk)
+    biases = (bq, bk)
     outputs = (out_0, out_1)
 
     with ExitStack() as ctx:
         consts = ctx.enter_context(tc.tile_pool(name="consts", bufs=1))
         raw_pool = ctx.enter_context(tc.tile_pool(name="raw", bufs=1))
         mx_pool = ctx.enter_context(tc.tile_pool(name="mx", bufs=1))
-        stage = ctx.enter_context(tc.tile_pool(name="stage", bufs=3))
+        stage = ctx.enter_context(tc.tile_pool(name="stage", bufs=4))
         out_pool = ctx.enter_context(tc.tile_pool(name="outp", bufs=CHUNKS))
         scratch = ctx.enter_context(tc.tile_pool(name="scratch", bufs=4))
         flip_psum = ctx.enter_context(tc.psum_pool(name="flip", bufs=4))
@@ -56,7 +59,7 @@ def tile_lorentzmultiheadattention_pa_kernel(tc, x_space, Wq, bq, Wk, bk, out_0,
         make_identity(nc, ident[:])
         ones = consts.tile([P, P], BF16)
         nc.vector.memset(ones[:], 1.0)
-        bias_rows = consts.tile([P, 2 * FEATURES], BF16)
+        bias_rows = consts.tile([P, 2, FEATURES], BF16)
         nc.vector.memset(bias_rows[:], 0.0)
 
         def load_x(unit):
@@ -82,16 +85,14 @@ def tile_lorentzmultiheadattention_pa_kernel(tc, x_space, Wq, bq, Wk, bk, out_0,
         raw_w = [None] * CHUNKS
         raw_x[0] = load_x(0)
         raw_w[0] = load_w(0)
-        nc.sync.dma_start(out=bias_rows[0:1, 0:FEATURES], in_=bq.unsqueeze(0))
-        nc.sync.dma_start(out=bias_rows[0:1, FEATURES : 2 * FEATURES], in_=bk.unsqueeze(0))
-        raw_x[1] = load_x(1)
-        raw_x[2] = load_x(2)
-        raw_w[1] = load_w(1)
-        raw_x[3] = load_x(3)
-        for chunk in range(2, CHUNKS):
+        for w in range(2):
+            nc.sync.dma_start(out=bias_rows[0:1, w, :], in_=biases[w].unsqueeze(0))
+        for unit in range(1, X_UNITS):
+            raw_x[unit] = load_x(unit)
+        for chunk in range(1, CHUNKS):
             raw_w[chunk] = load_w(chunk)
 
-        def flip(raw, share_with_scalar):
+        def flip(raw, split):
             words = raw[:].bitcast(F32)
             grouped = stage.tile([P, PASSES * UNIT_ROWS * PACK], BF16, align_bytes=64, tag="grouped")
             grouped_words = grouped[:].bitcast(F32).rearrange(
@@ -104,10 +105,10 @@ def tile_lorentzmultiheadattention_pa_kernel(tc, x_space, Wq, bq, Wk, bk, out_0,
                         first = b * ROW_WORDS + (g * HALVES + u) * P
                         nc.tensor.transpose(flipped[:, g, u, :], words[:, first : first + P], ident[:])
                 source = flipped[:].rearrange("p g u r -> p g r u")
-                if share_with_scalar and b == 0:
-                    nc.scalar.copy(out=grouped_words[:, :, b, :, :], in_=source)
-                else:
+                if split and b == 1:
                     nc.vector.tensor_copy(out=grouped_words[:, :, b, :, :], in_=source)
+                else:
+                    nc.scalar.copy(out=grouped_words[:, :, b, :, :], in_=source)
             return grouped
 
         def quantise(grouped, name):
@@ -120,73 +121,128 @@ def tile_lorentzmultiheadattention_pa_kernel(tc, x_space, Wq, bq, Wk, bk, out_0,
             )
             return codes, scales
 
+        bias = consts.tile([P, 2, FEATURES], BF16)
+
+        def spread_bias(w):
+            spread = acc_psum.tile([P, FEATURES], BF16, tag="acc")
+            for q in range(FEATURES // BANK):
+                cols = slice(q * BANK, (q + 1) * BANK)
+                nc.tensor.matmul(
+                    out=spread[:, cols], lhsT=ones[:], rhs=bias_rows[:, w, cols], start=True, stop=True
+                )
+            nc.scalar.copy(out=bias[:, w, :], in_=spread[:])
+
         x_mx = [None] * X_UNITS
         w_mx = [None] * CHUNKS
-        x_mx[0] = quantise(flip(raw_x[0], True), "x0")
-        w_mx[0] = quantise(flip(raw_w[0], True), "w0")
+        grouped_x = [None] * X_UNITS
+        grouped_w = [None] * CHUNKS
+        lifted = [None] * CHUNKS
+        norms = [None] * CHUNKS
+        stats = [None] * CHUNKS
 
-        bias = consts.tile([P, 2 * FEATURES], F32)
-        for q in range(2 * FEATURES // BANK):
-            spread = acc_psum.tile([P, BANK], F32, tag="acc")
-            cols = slice(q * BANK, (q + 1) * BANK)
-            nc.tensor.matmul(out=spread[:], lhsT=ones[:], rhs=bias_rows[:, cols], start=True, stop=True)
-            nc.scalar.copy(out=bias[:, cols], in_=spread[:])
+        def project(chunk, unit):
+            x_codes, x_scales = x_mx[unit]
+            w_codes, w_scales = w_mx[chunk]
+            acc = acc_psum.tile([P, BLOCKS, UNIT_ROWS], F32, tag="acc")
+            for b in range(BLOCKS):
+                tokens = slice(b * P, (b + 1) * P)
+                for g in range(PASSES):
+                    nc.tensor.matmul_mx(
+                        out=acc[:, b, :],
+                        lhsT=x_codes[:, g, tokens].bitcast(FP8X4),
+                        lhsT_scale=x_scales[:, g, tokens],
+                        rhs=w_codes[:, g, :].bitcast(FP8X4),
+                        rhs_scale=w_scales[:, g, :],
+                        start=(g == 0),
+                        stop=(g == PASSES - 1),
+                    )
+            return acc
 
-        for chunk in range(CHUNKS):
-            lifted = out_pool.tile([P, CHUNK_HEADS, J, LIFTED], F32, tag="lifted")
-            norms = out_pool.tile([P, CHUNK_HEADS, J], F32, tag="norms")
-            bias_chunk = bias[:, chunk * UNIT_ROWS : (chunk + 1) * UNIT_ROWS].rearrange(
+        def add_bias(chunk, unit, acc):
+            first = (chunk % W_UNITS) * UNIT_ROWS
+            bias_chunk = bias[:, chunk // W_UNITS, first : first + UNIT_ROWS].rearrange(
                 "p (h d) -> p h d", d=HEAD_DIM
             )
-            w_codes, w_scales = w_mx[chunk]
-            for unit in range(X_UNITS):
-                next_x = chunk == 0 and unit + 1 < X_UNITS
-                next_w = unit == 1 and chunk + 1 < CHUNKS
-                if next_x:
-                    grouped_x = flip(raw_x[unit + 1], True)
-                if next_w:
-                    grouped_w = flip(raw_w[chunk + 1], chunk == 0)
+            j0 = unit * BLOCKS
+            nc.vector.tensor_tensor(
+                out=lifted[chunk][:, :, j0 : j0 + BLOCKS, 1:LIFTED],
+                in0=acc[:].rearrange("p b (h d) -> p h b d", d=HEAD_DIM),
+                in1=bias_chunk.unsqueeze(2).to_broadcast([P, CHUNK_HEADS, BLOCKS, HEAD_DIM]),
+                op=ALU.add,
+            )
 
-                x_codes, x_scales = x_mx[unit]
-                acc = acc_psum.tile([P, BLOCKS, UNIT_ROWS], F32, tag="acc")
-                for b in range(BLOCKS):
-                    tokens = slice(b * P, (b + 1) * P)
-                    for g in range(PASSES):
-                        nc.tensor.matmul_mx(
-                            out=acc[:, b, :],
-                            lhsT=x_codes[:, g, tokens].bitcast(FP8X4),
-                            lhsT_scale=x_scales[:, g, tokens],
-                            rhs=w_codes[:, g, :].bitcast(FP8X4),
-                            rhs_scale=w_scales[:, g, :],
-                            start=(g == 0),
-                            stop=(g == PASSES - 1),
-                        )
-                j0 = unit * BLOCKS
-                nc.vector.tensor_tensor(
-                    out=lifted[:, :, j0 : j0 + BLOCKS, 1:LIFTED],
-                    in0=acc[:].rearrange("p b (h d) -> p h b d", d=HEAD_DIM),
-                    in1=bias_chunk.unsqueeze(2).to_broadcast([P, CHUNK_HEADS, BLOCKS, HEAD_DIM]),
-                    op=ALU.add,
+        def sum_squares(chunk, unit):
+            squares = scratch.tile([P, SCALAR_HEADS, BLOCKS, HEAD_DIM], F32, tag="squares")
+            for b in range(BLOCKS):
+                j = unit * BLOCKS + b
+                nc.vector.bn_stats(
+                    out=stats[chunk][:, j, :, :].rearrange("p h s -> p (h s)"),
+                    in_=lifted[chunk][:, SCALAR_HEADS:CHUNK_HEADS, j, 1:LIFTED].rearrange("p h d -> p d h"),
                 )
-                squares = scratch.tile([P, CHUNK_HEADS, BLOCKS, HEAD_DIM], F32, tag="squares")
-                for h in range(CHUNK_HEADS):
-                    for b in range(BLOCKS):
-                        nc.scalar.activation(
-                            out=squares[:, h, b, :],
-                            in_=lifted[:, h, j0 + b, 1:LIFTED],
-                            func=ACT.Square,
-                            accum_out=norms[:, h, j0 + b : j0 + b + 1],
-                        )
-                if next_x:
-                    x_mx[unit + 1] = quantise(grouped_x, "x%d" % (unit + 1))
-                if next_w:
-                    w_mx[chunk + 1] = quantise(grouped_w, "w%d" % (chunk + 1))
-            nc.scalar.activation(out=lifted[:, :, :, 0], in_=norms[:], func=ACT.Sqrt, bias=1.0)
+                for h in range(SCALAR_HEADS):
+                    nc.scalar.activation(
+                        out=squares[:, h, b, :],
+                        in_=lifted[chunk][:, h, j, 1:LIFTED],
+                        func=ACT.Square,
+                        accum_out=norms[chunk][:, h, j : j + 1],
+                    )
+
+        def square_means(chunk):
+            mean_sq = scratch.tile([P, J, 2], F32, tag="mean_sq")
+            nc.vector.scalar_tensor_tensor(
+                out=mean_sq[:],
+                in0=stats[chunk][:, :, :, 1],
+                scalar=float(HEAD_DIM),
+                in1=stats[chunk][:, :, :, 1],
+                op0=ALU.mult,
+                op1=ALU.mult,
+            )
+            return mean_sq
+
+        def finish(chunk, mean_sq):
+            nc.vector.tensor_tensor(
+                out=norms[chunk][:, SCALAR_HEADS:CHUNK_HEADS, :].rearrange("p h j -> p j h"),
+                in0=mean_sq[:],
+                in1=stats[chunk][:, :, :, 2],
+                op=ALU.add,
+            )
+            nc.scalar.activation(out=lifted[chunk][:, :, :, 0], in_=norms[chunk][:], func=ACT.Sqrt, bias=1.0)
             h0 = (chunk % W_UNITS) * CHUNK_HEADS
             for b in range(BATCH):
                 nc.sync.dma_start(
                     out=outputs[chunk // W_UNITS][b, h0 : h0 + CHUNK_HEADS].rearrange(
                         "h (p j) c -> p h (j c)", j=J
                     ),
-                    in_=lifted[b:P:BATCH].rearrange("p h j c -> p h (j c)"),
+                    in_=lifted[chunk][b:P:BATCH].rearrange("p h j c -> p h (j c)"),
                 )
+
+        x_mx[0] = quantise(flip(raw_x[0], True), "x0")
+        w_mx[0] = quantise(flip(raw_w[0], True), "w0")
+        spread_bias(0)
+        grouped_x[1] = flip(raw_x[1], False)
+
+        for step in range(STEPS + 2):
+            if step < STEPS:
+                chunk, unit = divmod(step, X_UNITS)
+                if unit == 0:
+                    lifted[chunk] = out_pool.tile([P, CHUNK_HEADS, J, LIFTED], F32, name="lifted", tag="lifted")
+                    norms[chunk] = out_pool.tile([P, CHUNK_HEADS, J], F32, name="norms", tag="norms")
+                    stats[chunk] = out_pool.tile([P, J, 2, 3], F32, name="stats", tag="stats")
+                if chunk == 0 and unit + 2 < X_UNITS:
+                    grouped_x[unit + 2] = flip(raw_x[unit + 2], False)
+                if chunk == 0 and unit + 1 < X_UNITS:
+                    x_mx[unit + 1] = quantise(grouped_x[unit + 1], "x%d" % (unit + 1))
+                if unit == 1 and chunk + 1 < CHUNKS:
+                    grouped_w[chunk + 1] = flip(raw_w[chunk + 1], False)
+                if unit == 3 and chunk + 1 < CHUNKS:
+                    w_mx[chunk + 1] = quantise(grouped_w[chunk + 1], "w%d" % (chunk + 1))
+                if step == X_UNITS:
+                    spread_bias(1)
+                add_bias(chunk, unit, project(chunk, unit))
+            closing = step >= 2 and (step - 2) % X_UNITS == X_UNITS - 1
+            if closing:
+                mean_sq = square_means((step - 2) // X_UNITS)
+            if 1 <= step <= STEPS:
+                sum_squares((step - 1) // X_UNITS, (step - 1) % X_UNITS)
+            if closing:
+                finish((step - 2) // X_UNITS, mean_sq)

@@ -10,6 +10,7 @@ U8 = mybir.dt.uint8
 FP8X4 = mybir.dt.float8_e4m3fn_x4
 ACT = mybir.ActivationFunctionType
 ALU = mybir.AluOpType
+AXIS = mybir.AxisListType
 
 P = 128
 BATCH, TOKENS, K = 2, 512, 1024
@@ -27,7 +28,7 @@ X_UNITS = J // BLOCKS
 CHUNK_HEADS = UNIT_ROWS // HEAD_DIM
 W_UNITS = FEATURES // UNIT_ROWS
 CHUNKS = 2 * W_UNITS
-SCALAR_HEADS = 2
+POOL_UNIT = 0
 STEPS = CHUNKS * X_UNITS
 BANK = 512
 
@@ -92,7 +93,7 @@ def tile_lorentzmultiheadattention_pa_kernel(tc, x_space, Wq, bq, Wk, bk, out_0,
         for chunk in range(1, CHUNKS):
             raw_w[chunk] = load_w(chunk)
 
-        def flip(raw, split):
+        def flip(raw):
             words = raw[:].bitcast(F32)
             grouped = stage.tile([P, PASSES * UNIT_ROWS * PACK], BF16, align_bytes=64, tag="grouped")
             grouped_words = grouped[:].bitcast(F32).rearrange(
@@ -105,10 +106,10 @@ def tile_lorentzmultiheadattention_pa_kernel(tc, x_space, Wq, bq, Wk, bk, out_0,
                         first = b * ROW_WORDS + (g * HALVES + u) * P
                         nc.tensor.transpose(flipped[:, g, u, :], words[:, first : first + P], ident[:])
                 source = flipped[:].rearrange("p g u r -> p g r u")
-                if split and b == 1:
-                    nc.vector.tensor_copy(out=grouped_words[:, :, b, :, :], in_=source)
-                else:
+                if b == 0:
                     nc.scalar.copy(out=grouped_words[:, :, b, :, :], in_=source)
+                else:
+                    nc.vector.tensor_copy(out=grouped_words[:, :, b, :, :], in_=source)
             return grouped
 
         def quantise(grouped, name):
@@ -138,7 +139,7 @@ def tile_lorentzmultiheadattention_pa_kernel(tc, x_space, Wq, bq, Wk, bk, out_0,
         grouped_w = [None] * CHUNKS
         lifted = [None] * CHUNKS
         norms = [None] * CHUNKS
-        stats = [None] * CHUNKS
+        pool_squares = [None] * CHUNKS
 
         def project(chunk, unit):
             x_codes, x_scales = x_mx[unit]
@@ -171,78 +172,76 @@ def tile_lorentzmultiheadattention_pa_kernel(tc, x_space, Wq, bq, Wk, bk, out_0,
                 op=ALU.add,
             )
 
-        def sum_squares(chunk, unit):
-            squares = scratch.tile([P, SCALAR_HEADS, BLOCKS, HEAD_DIM], F32, tag="squares")
-            for b in range(BLOCKS):
-                j = unit * BLOCKS + b
-                nc.vector.bn_stats(
-                    out=stats[chunk][:, j, :, :].rearrange("p h s -> p (h s)"),
-                    in_=lifted[chunk][:, SCALAR_HEADS:CHUNK_HEADS, j, 1:LIFTED].rearrange("p h d -> p d h"),
-                )
-                for h in range(SCALAR_HEADS):
+        def scalar_norms(chunk, heads, tokens):
+            squares = scratch.tile([P, len(heads), len(tokens), HEAD_DIM], F32, tag="squares")
+            for row, h in enumerate(heads):
+                for col, j in enumerate(tokens):
                     nc.scalar.activation(
-                        out=squares[:, h, b, :],
+                        out=squares[:, row, col, :],
                         in_=lifted[chunk][:, h, j, 1:LIFTED],
                         func=ACT.Square,
-                        accum_out=norms[chunk][:, h, j : j + 1],
+                        accum_out=norms[chunk][:, j, h : h + 1],
                     )
 
-        def square_means(chunk):
-            mean_sq = scratch.tile([P, J, 2], F32, tag="mean_sq")
-            nc.vector.scalar_tensor_tensor(
-                out=mean_sq[:],
-                in0=stats[chunk][:, :, :, 1],
-                scalar=float(HEAD_DIM),
-                in1=stats[chunk][:, :, :, 1],
-                op0=ALU.mult,
-                op1=ALU.mult,
-            )
-            return mean_sq
+        def pool_square(chunk):
+            j0 = POOL_UNIT * BLOCKS
+            vectors = lifted[chunk][:, :, j0 : j0 + BLOCKS, 1:LIFTED].rearrange("p h b d -> p b h d")
+            pool_squares[chunk] = scratch.tile([P, BLOCKS, CHUNK_HEADS, HEAD_DIM], F32, name="pool_sq", tag="pool_sq")
+            nc.gpsimd.tensor_tensor(out=pool_squares[chunk][:], in0=vectors, in1=vectors, op=ALU.mult)
 
-        def finish(chunk, mean_sq):
-            nc.vector.tensor_tensor(
-                out=norms[chunk][:, SCALAR_HEADS:CHUNK_HEADS, :].rearrange("p h j -> p j h"),
-                in0=mean_sq[:],
-                in1=stats[chunk][:, :, :, 2],
-                op=ALU.add,
+        def vector_norms(chunk):
+            j0 = POOL_UNIT * BLOCKS
+            nc.vector.tensor_reduce(
+                out=norms[chunk][:, j0 : j0 + BLOCKS, :], in_=pool_squares[chunk][:], axis=AXIS.X, op=ALU.add
             )
-            nc.scalar.activation(out=lifted[chunk][:, :, :, 0], in_=norms[chunk][:], func=ACT.Sqrt, bias=1.0)
-            h0 = (chunk % W_UNITS) * CHUNK_HEADS
+
+        def finish(chunk, heads):
+            h0, h1 = heads[0], heads[-1] + 1
+            nc.scalar.activation(
+                out=lifted[chunk][:, h0:h1, :, 0],
+                in_=norms[chunk][:, :, h0:h1].rearrange("p j h -> p h j"),
+                func=ACT.Sqrt,
+                bias=1.0,
+            )
+            first = (chunk % W_UNITS) * CHUNK_HEADS
             for b in range(BATCH):
                 nc.sync.dma_start(
-                    out=outputs[chunk // W_UNITS][b, h0 : h0 + CHUNK_HEADS].rearrange(
+                    out=outputs[chunk // W_UNITS][b, first + h0 : first + h1].rearrange(
                         "h (p j) c -> p h (j c)", j=J
                     ),
-                    in_=lifted[chunk][b:P:BATCH].rearrange("p h j c -> p h (j c)"),
+                    in_=lifted[chunk][b:P:BATCH, h0:h1].rearrange("p h j c -> p h (j c)"),
                 )
 
-        x_mx[0] = quantise(flip(raw_x[0], True), "x0")
-        w_mx[0] = quantise(flip(raw_w[0], True), "w0")
+        all_heads = list(range(CHUNK_HEADS))
+        x_mx[0] = quantise(flip(raw_x[0]), "x0")
+        w_mx[0] = quantise(flip(raw_w[0]), "w0")
         spread_bias(0)
-        grouped_x[1] = flip(raw_x[1], False)
+        grouped_x[1] = flip(raw_x[1])
 
-        for step in range(STEPS + 2):
-            if step < STEPS:
-                chunk, unit = divmod(step, X_UNITS)
-                if unit == 0:
-                    lifted[chunk] = out_pool.tile([P, CHUNK_HEADS, J, LIFTED], F32, name="lifted", tag="lifted")
-                    norms[chunk] = out_pool.tile([P, CHUNK_HEADS, J], F32, name="norms", tag="norms")
-                    stats[chunk] = out_pool.tile([P, J, 2, 3], F32, name="stats", tag="stats")
+        for chunk in range(CHUNKS):
+            lifted[chunk] = out_pool.tile([P, CHUNK_HEADS, J, LIFTED], F32, name="lifted", tag="lifted")
+            norms[chunk] = out_pool.tile([P, J, CHUNK_HEADS], F32, name="norms", tag="norms")
+            for unit in range(X_UNITS):
                 if chunk == 0 and unit + 2 < X_UNITS:
-                    grouped_x[unit + 2] = flip(raw_x[unit + 2], False)
+                    grouped_x[unit + 2] = flip(raw_x[unit + 2])
                 if chunk == 0 and unit + 1 < X_UNITS:
                     x_mx[unit + 1] = quantise(grouped_x[unit + 1], "x%d" % (unit + 1))
-                if unit == 1 and chunk + 1 < CHUNKS:
-                    grouped_w[chunk + 1] = flip(raw_w[chunk + 1], False)
-                if unit == 3 and chunk + 1 < CHUNKS:
-                    w_mx[chunk + 1] = quantise(grouped_w[chunk + 1], "w%d" % (chunk + 1))
-                if step == X_UNITS:
+                if unit == (X_UNITS - 2 if chunk == 0 else 0) and chunk + 1 < CHUNKS:
+                    grouped_w[chunk + 1] = flip(raw_w[chunk + 1])
+                if chunk == 1 and unit == 0:
                     spread_bias(1)
                 add_bias(chunk, unit, project(chunk, unit))
-            closing = step >= 2 and (step - 2) % X_UNITS == X_UNITS - 1
-            if closing:
-                mean_sq = square_means((step - 2) // X_UNITS)
-            if 1 <= step <= STEPS:
-                sum_squares((step - 1) // X_UNITS, (step - 1) % X_UNITS)
-            if closing:
-                finish((step - 2) // X_UNITS, mean_sq)
+                if unit == POOL_UNIT and chunk > 0:
+                    pool_square(chunk)
+                elif chunk + 1 < CHUNKS or unit + 1 < X_UNITS:
+                    scalar_norms(chunk, all_heads, list(range(unit * BLOCKS, (unit + 1) * BLOCKS)))
+            if chunk + 1 < CHUNKS:
+                w_mx[chunk + 1] = quantise(grouped_w[chunk + 1], "w%d" % (chunk + 1))
+            if chunk > 0:
+                vector_norms(chunk)
+            if chunk + 1 < CHUNKS:
+                finish(chunk, all_heads)
+
+        for h in all_heads:
+            scalar_norms(CHUNKS - 1, [h], list(range(J - BLOCKS, J)))
+            finish(CHUNKS - 1, [h])

@@ -82,18 +82,17 @@ def tile_lorentzmultiheadattention_pa_kernel(tc, x_space, Wq, bq, Wk, bk, out_0,
             )
             return raw
 
-        raw_x = [None] * X_UNITS
-        raw_w = [None] * CHUNKS
-        raw_x[0] = load_x(0)
-        raw_w[0] = load_w(0)
-        for w in range(2):
-            nc.sync.dma_start(out=bias_rows[0:1, w, :], in_=biases[w].unsqueeze(0))
-        for unit in range(1, X_UNITS):
-            raw_x[unit] = load_x(unit)
-        for chunk in range(1, CHUNKS):
-            raw_w[chunk] = load_w(chunk)
+        order = [("x", 0), ("w", 0)]
+        order.extend([("x", unit) for unit in range(1, X_UNITS)])
+        order.extend([("w", chunk) for chunk in range(1, CHUNKS)])
+        raw = {}
+        for kind, n in order:
+            raw[(kind, n)] = load_x(n) if kind == "x" else load_w(n)
+            if (kind, n) == ("w", 0):
+                for w in range(2):
+                    nc.sync.dma_start(out=bias_rows[0:1, w, :], in_=biases[w].unsqueeze(0))
 
-        def flip(raw):
+        def flip(raw, vector_helps=True):
             words = raw[:].bitcast(F32)
             grouped = stage.tile([P, PASSES * UNIT_ROWS * PACK], BF16, align_bytes=64, tag="grouped")
             grouped_words = grouped[:].bitcast(F32).rearrange(
@@ -106,13 +105,14 @@ def tile_lorentzmultiheadattention_pa_kernel(tc, x_space, Wq, bq, Wk, bk, out_0,
                         first = b * ROW_WORDS + (g * HALVES + u) * P
                         nc.tensor.transpose(flipped[:, g, u, :], words[:, first : first + P], ident[:])
                 source = flipped[:].rearrange("p g u r -> p g r u")
-                if b == 0:
-                    nc.scalar.copy(out=grouped_words[:, :, b, :, :], in_=source)
-                else:
+                if b == 1 and vector_helps:
                     nc.vector.tensor_copy(out=grouped_words[:, :, b, :, :], in_=source)
+                else:
+                    nc.scalar.copy(out=grouped_words[:, :, b, :, :], in_=source)
             return grouped
 
-        def quantise(grouped, name):
+        def quantise(grouped, key):
+            name = "%s%d" % key
             codes = mx_pool.tile([P, PASSES, UNIT_ROWS], U32, align_bytes=64, name="codes_" + name)
             scales = mx_pool.tile([P, PASSES, UNIT_ROWS], U8, align_bytes=64, name="scales_" + name)
             nc.vector.quantize_mx(
@@ -133,17 +133,14 @@ def tile_lorentzmultiheadattention_pa_kernel(tc, x_space, Wq, bq, Wk, bk, out_0,
                 )
             nc.scalar.copy(out=bias[:, w, :], in_=spread[:])
 
-        x_mx = [None] * X_UNITS
-        w_mx = [None] * CHUNKS
-        grouped_x = [None] * X_UNITS
-        grouped_w = [None] * CHUNKS
+        mx = {}
         lifted = [None] * CHUNKS
         norms = [None] * CHUNKS
         pool_squares = [None] * CHUNKS
 
         def project(chunk, unit):
-            x_codes, x_scales = x_mx[unit]
-            w_codes, w_scales = w_mx[chunk]
+            x_codes, x_scales = mx[("x", unit)]
+            w_codes, w_scales = mx[("w", chunk)]
             acc = acc_psum.tile([P, BLOCKS, UNIT_ROWS], F32, tag="acc")
             for b in range(BLOCKS):
                 tokens = slice(b * P, (b + 1) * P)
@@ -213,21 +210,22 @@ def tile_lorentzmultiheadattention_pa_kernel(tc, x_space, Wq, bq, Wk, bk, out_0,
                 )
 
         all_heads = list(range(CHUNK_HEADS))
-        x_mx[0] = quantise(flip(raw_x[0]), "x0")
-        w_mx[0] = quantise(flip(raw_w[0]), "w0")
+        for key in order[0:2]:
+            mx[key] = quantise(flip(raw[key]), key)
         spread_bias(0)
-        grouped_x[1] = flip(raw_x[1])
+        grouped = flip(raw[order[2]], vector_helps=False)
+        flipped, quantised = 3, 2
 
         for chunk in range(CHUNKS):
             lifted[chunk] = out_pool.tile([P, CHUNK_HEADS, J, LIFTED], F32, name="lifted", tag="lifted")
             norms[chunk] = out_pool.tile([P, J, CHUNK_HEADS], F32, name="norms", tag="norms")
             for unit in range(X_UNITS):
-                if chunk == 0 and unit + 2 < X_UNITS:
-                    grouped_x[unit + 2] = flip(raw_x[unit + 2])
-                if chunk == 0 and unit + 1 < X_UNITS:
-                    x_mx[unit + 1] = quantise(grouped_x[unit + 1], "x%d" % (unit + 1))
-                if unit == (X_UNITS - 2 if chunk == 0 else 0) and chunk + 1 < CHUNKS:
-                    grouped_w[chunk + 1] = flip(raw_w[chunk + 1])
+                if quantised < flipped and (chunk == 0 or unit == 0):
+                    mx[order[quantised]] = quantise(grouped, order[quantised])
+                    quantised += 1
+                if flipped < len(order) and (chunk == 0 or unit == 1):
+                    grouped = flip(raw[order[flipped]])
+                    flipped += 1
                 if chunk == 1 and unit == 0:
                     spread_bias(1)
                 add_bias(chunk, unit, project(chunk, unit))
@@ -235,8 +233,6 @@ def tile_lorentzmultiheadattention_pa_kernel(tc, x_space, Wq, bq, Wk, bk, out_0,
                     pool_square(chunk)
                 elif chunk + 1 < CHUNKS or unit + 1 < X_UNITS:
                     scalar_norms(chunk, all_heads, list(range(unit * BLOCKS, (unit + 1) * BLOCKS)))
-            if chunk + 1 < CHUNKS:
-                w_mx[chunk + 1] = quantise(grouped_w[chunk + 1], "w%d" % (chunk + 1))
             if chunk > 0:
                 vector_norms(chunk)
             if chunk + 1 < CHUNKS:

@@ -224,7 +224,7 @@ def tile_lorentzmultiheadattention_pa_kernel(tc, x_space, Wq, bq, Wk, bk, out_0,
                     mx[order[quantised]] = quantise(grouped, order[quantised])
                     quantised += 1
                 if flipped < len(order) and (chunk == 0 or unit == 1):
-                    grouped = flip(raw[order[flipped]])
+                    grouped = flip(raw[order[flipped]], vector_helps=(chunk % 2 == 0))
                     flipped += 1
                 if chunk == 1 and unit == 0:
                     spread_bias(1)

from contextlib import ExitStack

import concourse.mybir as mybir
from concourse.masks import make_identity

F32 = mybir.dt.float32
BF16 = mybir.dt.bfloat16
U32 = mybir.dt.uint32
U8 = mybir.dt.uint8
FP8X4 = mybir.dt.float8_e4m3fn_x4
ACT = mybir.ActivationFunctionType
ALU = mybir.AluOpType
AXIS = mybir.AxisListType

P = 128
BATCH, TOKENS, K = 2, 512, 1024
FEATURES, HEAD_DIM = 1024, 64
LIFTED = HEAD_DIM + 1
PACK = 4
K_PASS = P * PACK
PASSES = K // K_PASS
HALVES = 2
ROW_WORDS = K // 2
BLOCKS = 2
UNIT_ROWS = BLOCKS * P
J = BATCH * TOKENS // P
X_UNITS = J // BLOCKS
CHUNK_HEADS = UNIT_ROWS // HEAD_DIM
W_UNITS = FEATURES // UNIT_ROWS
CHUNKS = 2 * W_UNITS
POOL_UNIT = 0
STEPS = CHUNKS * X_UNITS
BANK = 512

FLOPS = 2 * BATCH * TOKENS * K * 2 * FEATURES


def tile_lorentzmultiheadattention_pa_kernel(tc, x_space, Wq, bq, Wk, bk, out_0, out_1):
    nc = tc.nc
    weights = (Wq, Wk)
    biases = (bq, bk)
    outputs = (out_0, out_1)

    with ExitStack() as ctx:
        consts = ctx.enter_context(tc.tile_pool(name="consts", bufs=1))
        raw_pool = ctx.enter_context(tc.tile_pool(name="raw", bufs=1))
        mx_pool = ctx.enter_context(tc.tile_pool(name="mx", bufs=1))
        stage = ctx.enter_context(tc.tile_pool(name="stage", bufs=4))
        out_pool = ctx.enter_context(tc.tile_pool(name="outp", bufs=CHUNKS))
        scratch = ctx.enter_context(tc.tile_pool(name="scratch", bufs=4))
        flip_psum = ctx.enter_context(tc.psum_pool(name="flip", bufs=4))
        acc_psum = ctx.enter_context(tc.psum_pool(name="acc", bufs=4))
        ctx.enter_context(tc.manual_schedule())

        one = consts.tile([P, 1], F32)
        nc.vector.memset(one[:], 1.0)
        root = consts.tile([P, 1], F32)
        nc.scalar.activation(out=root[:], in_=one[:], func=ACT.Sqrt)
        ident = consts.tile([P, P], F32)
        make_identity(nc, ident[:])
        ones = consts.tile([P, P], BF16)
        nc.vector.memset(ones[:], 1.0)
        bias_rows = consts.tile([P, 2, FEATURES], BF16)
        nc.vector.memset(bias_rows[:], 0.0)

        def load_x(unit):
            raw = raw_pool.tile([P, BLOCKS * K], BF16, name="raw_x%d" % unit)
            for b in range(BATCH):
                rows = x_space[b].rearrange("(p j) k -> p (j k)", j=J)
                nc.sync.dma_start(
                    out=raw[b:P:BATCH, :],
                    in_=rows[:, unit * BLOCKS * K : (unit + 1) * BLOCKS * K],
                )
            return raw

        def load_w(chunk):
            raw = raw_pool.tile([P, BLOCKS * K], BF16, name="raw_w%d" % chunk)
            rows = weights[chunk // W_UNITS].rearrange("(c b r) k -> c r b k", b=BLOCKS, r=P)
            nc.sync.dma_start(
                out=raw[:].rearrange("p (b k) -> p b k", b=BLOCKS),
                in_=rows[chunk % W_UNITS],
            )
            return raw

        order = [("x", 0), ("w", 0)]
        order.extend([("x", unit) for unit in range(1, X_UNITS)])
        order.extend([("w", chunk) for chunk in range(1, CHUNKS)])
        raw = {}
        for kind, n in order:
            raw[(kind, n)] = load_x(n) if kind == "x" else load_w(n)
            if (kind, n) == ("w", 0):
                for w in range(2):
                    nc.sync.dma_start(out=bias_rows[0:1, w, :], in_=biases[w].unsqueeze(0))

        def flip(raw, vector_helps=True):
            words = raw[:].bitcast(F32)
            grouped = stage.tile([P, PASSES * UNIT_ROWS * PACK], BF16, align_bytes=64, tag="grouped")
            grouped_words = grouped[:].bitcast(F32).rearrange(
                "p (g b r u) -> p g b r u", g=PASSES, b=BLOCKS, u=HALVES
            )
            for b in range(BLOCKS):
                flipped = flip_psum.tile([P, PASSES, HALVES, P], F32, tag="flip")
                for g in range(PASSES):
                    for u in range(HALVES):
                        first = b * ROW_WORDS + (g * HALVES + u) * P
                        nc.tensor.transpose(flipped[:, g, u, :], words[:, first : first + P], ident[:])
                source = flipped[:].rearrange("p g u r -> p g r u")
                if b == 1 and vector_helps:
                    nc.vector.tensor_copy(out=grouped_words[:, :, b, :, :], in_=source)
                else:
                    nc.scalar.copy(out=grouped_words[:, :, b, :, :], in_=source)
            return grouped

        def quantise(grouped, key):
            name = "%s%d" % key
            codes = mx_pool.tile([P, PASSES, UNIT_ROWS], U32, align_bytes=64, name="codes_" + name)
            scales = mx_pool.tile([P, PASSES, UNIT_ROWS], U8, align_bytes=64, name="scales_" + name)
            nc.vector.quantize_mx(
                out=codes[:].rearrange("p g r -> p (g r)").bitcast(FP8X4),
                scales=scales[:].rearrange("p g r -> p (g r)"),
                in_=grouped[:],
            )
            return codes, scales

        bias = consts.tile([P, 2, FEATURES], BF16)

        def spread_bias(w):
            spread = acc_psum.tile([P, FEATURES], BF16, tag="acc")
            for q in range(FEATURES // BANK):
                cols = slice(q * BANK, (q + 1) * BANK)
                nc.tensor.matmul(
                    out=spread[:, cols], lhsT=ones[:], rhs=bias_rows[:, w, cols], start=True, stop=True
                )
            nc.scalar.copy(out=bias[:, w, :], in_=spread[:])

        mx = {}
        lifted = [None] * CHUNKS
        norms = [None] * CHUNKS
        pool_squares = [None] * CHUNKS

        def project(chunk, unit):
            x_codes, x_scales = mx[("x", unit)]
            w_codes, w_scales = mx[("w", chunk)]
            acc = acc_psum.tile([P, BLOCKS, UNIT_ROWS], F32, tag="acc")
            for b in range(BLOCKS):
                tokens = slice(b * P, (b + 1) * P)
                for g in range(PASSES):
                    nc.tensor.matmul_mx(
                        out=acc[:, b, :],
                        lhsT=x_codes[:, g, tokens].bitcast(FP8X4),
                        lhsT_scale=x_scales[:, g, tokens],
                        rhs=w_codes[:, g, :].bitcast(FP8X4),
                        rhs_scale=w_scales[:, g, :],
                        start=(g == 0),
                        stop=(g == PASSES - 1),
                    )
            return acc

        def add_bias(chunk, unit, acc):
            first = (chunk % W_UNITS) * UNIT_ROWS
            bias_chunk = bias[:, chunk // W_UNITS, first : first + UNIT_ROWS].rearrange(
                "p (h d) -> p h d", d=HEAD_DIM
            )
            j0 = unit * BLOCKS
            nc.vector.tensor_tensor(
                out=lifted[chunk][:, :, j0 : j0 + BLOCKS, 1:LIFTED],
                in0=acc[:].rearrange("p b (h d) -> p h b d", d=HEAD_DIM),
                in1=bias_chunk.unsqueeze(2).to_broadcast([P, CHUNK_HEADS, BLOCKS, HEAD_DIM]),
                op=ALU.add,
            )

        def scalar_norms(chunk, heads, tokens):
            squares = scratch.tile([P, len(heads), len(tokens), HEAD_DIM], F32, tag="squares")
            for row, h in enumerate(heads):
                for col, j in enumerate(tokens):
                    nc.scalar.activation(
                        out=squares[:, row, col, :],
                        in_=lifted[chunk][:, h, j, 1:LIFTED],
                        func=ACT.Square,
                        accum_out=norms[chunk][:, j, h : h + 1],
                    )

        def pool_square(chunk):
            j0 = POOL_UNIT * BLOCKS
            vectors = lifted[chunk][:, :, j0 : j0 + BLOCKS, 1:LIFTED].rearrange("p h b d -> p b h d")
            pool_squares[chunk] = scratch.tile([P, BLOCKS, CHUNK_HEADS, HEAD_DIM], F32, name="pool_sq", tag="pool_sq")
            nc.gpsimd.tensor_tensor(out=pool_squares[chunk][:], in0=vectors, in1=vectors, op=ALU.mult)

        def vector_norms(chunk):
            j0 = POOL_UNIT * BLOCKS
            nc.vector.tensor_reduce(
                out=norms[chunk][:, j0 : j0 + BLOCKS, :], in_=pool_squares[chunk][:], axis=AXIS.X, op=ALU.add
            )

        def finish(chunk, heads):
            h0, h1 = heads[0], heads[-1] + 1
            nc.scalar.activation(
                out=lifted[chunk][:, h0:h1, :, 0],
                in_=norms[chunk][:, :, h0:h1].rearrange("p j h -> p h j"),
                func=ACT.Sqrt,
                bias=1.0,
            )
            first = (chunk % W_UNITS) * CHUNK_HEADS
            for b in range(BATCH):
                nc.sync.dma_start(
                    out=outputs[chunk // W_UNITS][b, first + h0 : first + h1].rearrange(
                        "h (p j) c -> p h (j c)", j=J
                    ),
                    in_=lifted[chunk][b:P:BATCH, h0:h1].rearrange("p h j c -> p h (j c)"),
                )

        all_heads = list(range(CHUNK_HEADS))
        for key in order[0:2]:
            mx[key] = quantise(flip(raw[key]), key)
        spread_bias(0)
        grouped = flip(raw[order[2]], vector_helps=False)
        flipped, quantised = 3, 2

        for chunk in range(CHUNKS):
            lifted[chunk] = out_pool.tile([P, CHUNK_HEADS, J, LIFTED], F32, name="lifted", tag="lifted")
            norms[chunk] = out_pool.tile([P, J, CHUNK_HEADS], F32, name="norms", tag="norms")
            for unit in range(X_UNITS):
                if quantised < flipped and (chunk == 0 or unit == 0):
                    mx[order[quantised]] = quantise(grouped, order[quantised])
                    quantised += 1
                if flipped < len(order) and (chunk == 0 or unit == 1):
                    grouped = flip(raw[order[flipped]], vector_helps=(chunk % 2 == 0))
                    flipped += 1
                if chunk == 1 and unit == 0:
                    spread_bias(1)
                add_bias(chunk, unit, project(chunk, unit))
                if unit == POOL_UNIT and chunk > 0:
                    pool_square(chunk)
                elif chunk + 1 < CHUNKS or unit + 1 < X_UNITS:
                    scalar_norms(chunk, all_heads, list(range(unit * BLOCKS, (unit + 1) * BLOCKS)))
            if chunk > 0:
                vector_norms(chunk)
            if chunk + 1 < CHUNKS:
                finish(chunk, all_heads)

        for h in all_heads:
            scalar_norms(CHUNKS - 1, [h], list(range(J - BLOCKS, J)))
            finish(CHUNKS - 1, [h])
